import numpy as np
import ml_dtypes


def mxq(x, axis, fmt="e4m3"):
    dtype, down = {"e4m3": (ml_dtypes.float8_e4m3fn, 7), "e5m2": (ml_dtypes.float8_e5m2, 14)}[fmt]
    v = np.moveaxis(np.asarray(x, np.float32).astype(ml_dtypes.bfloat16).astype(np.float64), axis, -1)
    blocks = v.reshape(v.shape[:-1] + (-1, 32))
    amax = np.abs(blocks).max(-1, keepdims=True)
    byte = np.maximum(np.where(amax > 0, np.frexp(amax)[1] - 1 + 127, 0) - down, 1)
    scale = np.exp2(byte - 127.0)
    codes = (blocks / scale).astype(np.float32).astype(dtype).astype(np.float64)
    return np.moveaxis((codes * scale).reshape(v.shape), -1, axis)


WIDE = False


def mx_kscale(k):
    if not WIDE:
        return np.ones(k)
    levels = np.array([30, -30])
    if k % 512:
        return np.exp2(np.random.permutation(np.resize(levels, k // 32))).repeat(32)
    a = np.empty((k // 512, 16))
    for p in range(k // 512):
        a[p, :8] = np.random.permutation(np.resize(levels, 8))
        for g in range(8):
            far = levels[np.abs(levels - a[p, g]) >= 10]
            a[p, g + 8] = far[np.random.randint(len(far))]
    return np.exp2(a.ravel()).repeat(32)


BF16 = ml_dtypes.bfloat16


def bf(x):
    return np.asarray(x, np.float32).astype(BF16)


def f64(x):
    return np.asarray(x).astype(np.float64)


B, IMG, P0, P1, C, F = 2, 512, 8, 16, 2, 512
E0, E1 = IMG // P0, IMG // P1
N0, N1 = E0 * E0, E1 * E1
D0, D1 = P0 * P0 * C, P1 * P1 * C


def setup_inputs():
    s = mx_kscale(D1)
    flat = np.random.standard_normal((B, N1, D1)) * s
    img = flat.reshape(B, E1, E1, P1, P1, C).transpose(0, 1, 3, 2, 4, 5).reshape(B, IMG, IMG, C)
    encoded = img.reshape(B, E0, P0, E0, P0, C).transpose(0, 1, 3, 2, 4, 5).reshape(B, N0, D0)
    return {"encoded": bf(encoded),
            "W": bf(np.random.standard_normal((D1, F)) / np.sqrt(D1) / s[:, None]),
            "b": bf(np.random.standard_normal(F) * 0.3),
            "pos_emb": bf(np.random.standard_normal((N1, F)) * 0.5)}


def reference(encoded, W, b, pos_emb):
    x = f64(encoded).reshape(-1, E0, E0, P0, P0, C)
    img = x.transpose(0, 1, 3, 2, 4, 5).reshape(-1, IMG, IMG, C)
    new_patches = img.reshape(-1, E1, P1, E1, P1, C).transpose(0, 1, 3, 2, 4, 5)
    flat = new_patches.reshape(-1, N1, D1)
    return (mxq(flat, 2, "e5m2") @ mxq(f64(W), 0, "e4m3")) + f64(b) + f64(pos_emb)

@@ -1,0 +1,190 @@
+from contextlib import ExitStack
+
+import concourse.mybir as mybir
+from concourse.masks import make_identity
+
+F32 = mybir.dt.float32
+BF16 = mybir.dt.bfloat16
+U32 = mybir.dt.uint32
+U8 = mybir.dt.uint8
+E4M3 = mybir.dt.float8_e4m3fn_x4
+E5M2 = mybir.dt.float8_e5m2_x4
+ADD = mybir.AluOpType.add
+
+P = 128
+IMAGES = 2
+TILES = 8
+K = 512
+F = 512
+FLOPS = 2 * IMAGES * TILES * P * K * F
+
+LOAD_GROUPS = ((0, 1), (1, 2), (2, 4), (4, 8))
+
+
+def tile_resampling_kernel(tc, encoded, W, b, pos_emb, out):
+    nc = tc.nc
+    with ExitStack() as ctx:
+        keep = ctx.enter_context(tc.tile_pool(name="keep", bufs=1))
+        stage = ctx.enter_context(tc.tile_pool(name="stage", bufs=4))
+        pair = ctx.enter_context(tc.tile_pool(name="pair", bufs=2))
+        ps_bias = ctx.enter_context(tc.psum_pool(name="ps_bias", bufs=1))
+        ps_turn = ctx.enter_context(tc.psum_pool(name="ps_turn", bufs=3))
+        ps_acc = ctx.enter_context(tc.psum_pool(name="ps_acc", bufs=4))
+        ctx.enter_context(tc.manual_schedule())
+
+        ident = keep.tile([P, P], F32, align_bytes=64)
+        b_rows = keep.tile([P, 4], BF16, align_bytes=64)
+        b_all = keep.tile([P, F], BF16, align_bytes=64)
+        w_raw = keep.tile([P, 4, F], BF16, align_bytes=64)
+        w_grouped = keep.tile([P, F, 4], BF16, align_bytes=64)
+        w_codes = keep.tile([P, F], U32, align_bytes=64)
+        w_scales = keep.tile([P, F], U8, align_bytes=64)
+        pos = keep.tile([P, TILES, F], BF16, align_bytes=64)
+        result = keep.tile([P, IMAGES, TILES, F], F32, align_bytes=64)
+        b_turned = ps_bias.tile([P, 2, P], F32)
+
+        make_identity(nc, ident[:])
+
+        w_view = W.rearrange("(g u w e) f -> u g w (e f)", g=16, u=2, w=8, e=2)
+        pos_view = pos_emb.rearrange("(p j) f -> p j f", j=TILES)
+        x_raw = {}
+
+        def load_x(lo, hi):
+            raw = keep.tile([P, IMAGES, 2, (hi - lo) * 256], BF16, name="x_raw_%d" % lo, align_bytes=64)
+            for image in range(IMAGES):
+                rows = encoded[image].rearrange("(y a h t) d -> a y h (t d)", y=32, a=2, h=4, t=16)
+                for a in range(2):
+                    nc.sync.dma_start(out=raw[:, image, a, :], in_=rows[a][:, :, lo * 256 : hi * 256])
+            for j in range(lo, hi):
+                x_raw[j] = raw[:, :, :, (j - lo) * 256 : (j - lo + 1) * 256]
+
+        def load_pos(lo, hi):
+            nc.sync.dma_start(out=pos[:, lo:hi, :], in_=pos_view[:, lo:hi, :])
+
+        nc.sync.dma_start(out=b_rows[:], in_=b.rearrange("(p c) -> p c", c=4))
+        for u in range(2):
+            nc.sync.dma_start(out=w_raw[:, 2 * u : 2 * u + 2, :].rearrange("p e f -> p (e f)"), in_=w_view[u])
+        load_x(0, 1)
+        load_x(1, 2)
+        load_pos(0, 2)
+        load_x(2, 4)
+        load_pos(2, 4)
+        load_x(4, 8)
+        load_pos(4, 8)
+
+        ordered = {}
+        turned = {}
+        grouped = {}
+        codes = {}
+        scales = {}
+        acc = {}
+        pos_b = {}
+
+        def reorder(j):
+            t = stage.tile([P, IMAGES, 2, 2, 64], F32, name="ordered", align_bytes=64)
+            ordered[j] = t
+            src = x_raw[j].bitcast(F32)
+            for image in range(IMAGES):
+                nc.scalar.copy(out=t[:, image, :, :, :], in_=src[:, image, :, :].rearrange("p a (u w) -> p u a w", w=64))
+
+        def turn(j):
+            t = ps_turn.tile([P, IMAGES, 2, P], F32, name="turned")
+            turned[j] = t
+            for image in range(IMAGES):
+                for u in range(2):
+                    nc.tensor.transpose(
+                        t[:, image, u, :], ordered[j][:, image, u, :, :].rearrange("p a w -> p (a w)"), ident[:]
+                    )
+
+        def group(j):
+            t = stage.tile([P, IMAGES * P * 4], BF16, name="grouped", align_bytes=64)
+            grouped[j] = t
+            dst = t[:].bitcast(F32).rearrange("p (i m u) -> p i m u", i=IMAGES, u=2)
+            nc.scalar.copy(out=dst, in_=turned[j][:].rearrange("p i u m -> p i m u"))
+
+        def quantize(j):
+            c = stage.tile([P, IMAGES * P], U32, name="x_codes", align_bytes=64)
+            e = stage.tile([P, IMAGES * P], U8, name="x_scales", align_bytes=64)
+            codes[j] = c
+            scales[j] = e
+            nc.vector.quantize_mx(out=c[:].bitcast(E5M2), scales=e[:], in_=grouped[j][:])
+
+        def multiply(j):
+            for image in range(IMAGES):
+                t = ps_acc.tile([P, F], F32, name="acc")
+                acc[j, image] = t
+                cols = slice(image * P, (image + 1) * P)
+                nc.tensor.matmul_mx(
+                    out=t[:],
+                    lhsT=codes[j][:, cols].bitcast(E5M2),
+                    lhsT_scale=scales[j][:, cols],
+                    rhs=w_codes[:].bitcast(E4M3),
+                    rhs_scale=w_scales[:],
+                    start=True,
+                    stop=True,
+                )
+
+        def add_bias(j):
+            t = pair.tile([P, F], F32, name="pos_b", align_bytes=64)
+            pos_b[j] = t
+            if j == 0:
+                nc.vector.tensor_tensor(
+                    out=t[:].rearrange("p (n u e) -> p n u e", u=2, e=2),
+                    in0=pos[:, j, :].rearrange("p (n u e) -> p n u e", u=2, e=2),
+                    in1=b_turned[:].bitcast(BF16).rearrange("p u (n e) -> p n u e", e=2),
+                    op=ADD,
+                )
+            else:
+                nc.gpsimd.tensor_tensor(out=t[:], in0=pos[:, j, :], in1=b_all[:], op=ADD)
+
+        def finish(j):
+            for image in range(IMAGES):
+                nc.vector.tensor_tensor(out=result[:, image, j, :], in0=acc[j, image][:], in1=pos_b[j][:], op=ADD)
+                nc.sync.dma_start(
+                    out=out[image].rearrange("(p j) f -> p j f", j=TILES)[:, j, :], in_=result[:, image, j, :]
+                )
+
+        b_words = b_rows[:].bitcast(F32)
+        for u in range(2):
+            nc.tensor.transpose(b_turned[:, u, :], b_words[:, u : u + 1].to_broadcast([P, P]), ident[:])
+
+        half = F // 2
+        for h in range(2):
+            cols = slice(h * half, (h + 1) * half)
+            nc.vector.tensor_copy(
+                out=w_grouped[:, cols, :].rearrange("p (c i) t -> p c t i", i=4),
+                in_=w_raw[:, :, cols].rearrange("p t (c i) -> p c t i", i=4),
+            )
+        for h in range(2):
+            cols = slice(h * half, (h + 1) * half)
+            nc.vector.quantize_mx(
+                out=w_codes[:, cols].bitcast(E4M3),
+                scales=w_scales[:, cols],
+                in_=w_grouped[:, cols, :].rearrange("p f t -> p (f t)"),
+            )
+
+        for j in range(2):
+            reorder(j)
+            turn(j)
+        for j in range(2):
+            group(j)
+        quantize(0)
+        add_bias(0)
+        nc.scalar.copy(
+            out=b_all[:].bitcast(F32).rearrange("p (n u) -> p n u", u=2),
+            in_=b_turned[:].rearrange("p u n -> p n u"),
+        )
+        reorder(2)
+
+        for j in range(TILES):
+            multiply(j)
+            if j + 2 < TILES:
+                turn(j + 2)
+            if j + 1 < TILES:
+                quantize(j + 1)
+                add_bias(j + 1)
+            if j + 3 < TILES:
+                reorder(j + 3)
+            if j + 2 < TILES:
+                group(j + 2)
+            finish(j)

@@ -44,6 +44,8 @@ def tile_resampling_kernel(tc, encoded, W, b, pos_emb, out):
         b_turned = ps_bias.tile([P, 2, P], F32)
 
         make_identity(nc, ident[:])
+        warm = keep.tile([P, 1], F32, align_bytes=64)
+        nc.scalar.copy(out=warm[:], in_=ident[:, 0:1])
 
         w_view = W.rearrange("(g u w e) f -> u g w (e f)", g=16, u=2, w=8, e=2)
         pos_view = pos_emb.rearrange("(p j) f -> p j f", j=TILES)

@@ -16,9 +16,14 @@ IMAGES = 2
 TILES = 8
 K = 512
 F = 512
+STEPS = TILES + 1
 FLOPS = 2 * IMAGES * TILES * P * K * F
 
-LOAD_GROUPS = ((0, 1), (1, 2), (2, 4), (4, 8))
+W_HALF = F // 2
+
+
+def step_tiles(s):
+    return [(image, s - image) for image in range(IMAGES) if 0 <= s - image < TILES]
 
 
 def tile_resampling_kernel(tc, encoded, W, b, pos_emb, out):
@@ -26,7 +31,7 @@ def tile_resampling_kernel(tc, encoded, W, b, pos_emb, out):
     with ExitStack() as ctx:
         keep = ctx.enter_context(tc.tile_pool(name="keep", bufs=1))
         stage = ctx.enter_context(tc.tile_pool(name="stage", bufs=4))
-        pair = ctx.enter_context(tc.tile_pool(name="pair", bufs=2))
+        pair = ctx.enter_context(tc.tile_pool(name="pair", bufs=3))
         ps_bias = ctx.enter_context(tc.psum_pool(name="ps_bias", bufs=1))
         ps_turn = ctx.enter_context(tc.psum_pool(name="ps_turn", bufs=3))
         ps_acc = ctx.enter_context(tc.psum_pool(name="ps_acc", bufs=4))
@@ -47,31 +52,34 @@ def tile_resampling_kernel(tc, encoded, W, b, pos_emb, out):
         warm = keep.tile([P, 1], F32, align_bytes=64)
         nc.scalar.copy(out=warm[:], in_=ident[:, 0:1])
 
-        w_view = W.rearrange("(g u w e) f -> u g w (e f)", g=16, u=2, w=8, e=2)
+        w_view = W.rearrange("(p t) f -> p t f", t=4)
         pos_view = pos_emb.rearrange("(p j) f -> p j f", j=TILES)
         x_raw = {}
 
-        def load_x(lo, hi):
-            raw = keep.tile([P, IMAGES, 2, (hi - lo) * 256], BF16, name="x_raw_%d" % lo, align_bytes=64)
-            for image in range(IMAGES):
-                rows = encoded[image].rearrange("(y a h t) d -> a y h (t d)", y=32, a=2, h=4, t=16)
-                for a in range(2):
-                    nc.sync.dma_start(out=raw[:, image, a, :], in_=rows[a][:, :, lo * 256 : hi * 256])
+        def load_x(image, lo, hi):
+            raw = keep.tile([P, 2, (hi - lo) * 256], BF16, name="x_raw_%d_%d" % (image, lo), align_bytes=64)
+            rows = encoded[image].rearrange("(y a h t) d -> a y h (t d)", y=32, a=2, h=4, t=16)
+            for a in range(2):
+                nc.sync.dma_start(out=raw[:, a, :], in_=rows[a][:, :, lo * 256 : hi * 256])
             for j in range(lo, hi):
-                x_raw[j] = raw[:, :, :, (j - lo) * 256 : (j - lo + 1) * 256]
+                x_raw[image, j] = raw[:, :, (j - lo) * 256 : (j - lo + 1) * 256]
 
         def load_pos(lo, hi):
             nc.sync.dma_start(out=pos[:, lo:hi, :], in_=pos_view[:, lo:hi, :])
 
+        load_x(0, 0, 1)
+        nc.sync.dma_start(out=w_raw[:], in_=w_view)
         nc.sync.dma_start(out=b_rows[:], in_=b.rearrange("(p c) -> p c", c=4))
-        for u in range(2):
-            nc.sync.dma_start(out=w_raw[:, 2 * u : 2 * u + 2, :].rearrange("p e f -> p (e f)"), in_=w_view[u])
-        load_x(0, 1)
-        load_x(1, 2)
+        load_x(0, 1, 2)
+        load_x(1, 0, 1)
+        load_x(0, 2, 3)
+        load_x(1, 1, 2)
         load_pos(0, 2)
-        load_x(2, 4)
+        load_x(0, 3, 5)
+        load_x(1, 2, 4)
         load_pos(2, 4)
-        load_x(4, 8)
+        load_x(0, 5, 8)
+        load_x(1, 4, 8)
         load_pos(4, 8)
 
         ordered = {}
@@ -82,44 +90,45 @@ def tile_resampling_kernel(tc, encoded, W, b, pos_emb, out):
         acc = {}
         pos_b = {}
 
-        def reorder(j):
-            t = stage.tile([P, IMAGES, 2, 2, 64], F32, name="ordered", align_bytes=64)
-            ordered[j] = t
-            src = x_raw[j].bitcast(F32)
-            for image in range(IMAGES):
-                nc.scalar.copy(out=t[:, image, :, :, :], in_=src[:, image, :, :].rearrange("p a (u w) -> p u a w", w=64))
-
-        def turn(j):
-            t = ps_turn.tile([P, IMAGES, 2, P], F32, name="turned")
-            turned[j] = t
-            for image in range(IMAGES):
+        def reorder(s):
+            t = stage.tile([P, IMAGES, 2, P], F32, name="ordered", align_bytes=64)
+            ordered[s] = t
+            for d, key in enumerate(step_tiles(s)):
+                words = x_raw[key].bitcast(F32).rearrange("p a (c r q u) -> p u a r c q", c=2, r=8, u=2)
                 for u in range(2):
-                    nc.tensor.transpose(
-                        t[:, image, u, :], ordered[j][:, image, u, :, :].rearrange("p a w -> p (a w)"), ident[:]
-                    )
+                    nc.scalar.copy(out=t[:, d, u, :].rearrange("p (a r c q) -> p a r c q", a=2, r=8, c=2), in_=words[:, u])
 
-        def group(j):
+        def turn(s):
+            t = ps_turn.tile([P, IMAGES, 2, P], F32, name="turned")
+            turned[s] = t
+            for d in range(len(step_tiles(s))):
+                for u in range(2):
+                    nc.tensor.transpose(t[:, d, u, :], ordered[s][:, d, u, :], ident[:])
+
+        def group(s):
+            n = len(step_tiles(s))
             t = stage.tile([P, IMAGES * P * 4], BF16, name="grouped", align_bytes=64)
-            grouped[j] = t
-            dst = t[:].bitcast(F32).rearrange("p (i m u) -> p i m u", i=IMAGES, u=2)
-            nc.scalar.copy(out=dst, in_=turned[j][:].rearrange("p i u m -> p i m u"))
+            grouped[s] = t[:, : n * P * 4]
+            dst = grouped[s].bitcast(F32).rearrange("p (d m u) -> p d m u", d=n, u=2)
+            nc.scalar.copy(out=dst, in_=turned[s][:, :n, :, :].rearrange("p d u m -> p d m u"))
 
-        def quantize(j):
+        def quantize(s):
+            n = len(step_tiles(s))
             c = stage.tile([P, IMAGES * P], U32, name="x_codes", align_bytes=64)
             e = stage.tile([P, IMAGES * P], U8, name="x_scales", align_bytes=64)
-            codes[j] = c
-            scales[j] = e
-            nc.vector.quantize_mx(out=c[:].bitcast(E5M2), scales=e[:], in_=grouped[j][:])
+            codes[s] = c
+            scales[s] = e
+            nc.vector.quantize_mx(out=c[:, : n * P].bitcast(E5M2), scales=e[:, : n * P], in_=grouped[s])
 
-        def multiply(j):
-            for image in range(IMAGES):
+        def multiply(s):
+            for d, key in enumerate(step_tiles(s)):
                 t = ps_acc.tile([P, F], F32, name="acc")
-                acc[j, image] = t
-                cols = slice(image * P, (image + 1) * P)
+                acc[key] = t
+                cols = slice(d * P, (d + 1) * P)
                 nc.tensor.matmul_mx(
                     out=t[:],
-                    lhsT=codes[j][:, cols].bitcast(E5M2),
-                    lhsT_scale=scales[j][:, cols],
+                    lhsT=codes[s][:, cols].bitcast(E5M2),
+                    lhsT_scale=scales[s][:, cols],
                     rhs=w_codes[:].bitcast(E4M3),
                     rhs_scale=w_scales[:],
                     start=True,
@@ -139,54 +148,62 @@ def tile_resampling_kernel(tc, encoded, W, b, pos_emb, out):
             else:
                 nc.gpsimd.tensor_tensor(out=t[:], in0=pos[:, j, :], in1=b_all[:], op=ADD)
 
-        def finish(j):
-            for image in range(IMAGES):
-                nc.vector.tensor_tensor(out=result[:, image, j, :], in0=acc[j, image][:], in1=pos_b[j][:], op=ADD)
-                nc.sync.dma_start(
-                    out=out[image].rearrange("(p j) f -> p j f", j=TILES)[:, j, :], in_=result[:, image, j, :]
+        def finish(image, j):
+            rows = out[image].rearrange("(p j) f -> p j f", j=TILES)
+            parts = 2 if (image, j) == (IMAGES - 1, TILES - 1) else 1
+            for part in range(parts):
+                cols = slice(part * F // parts, (part + 1) * F // parts)
+                nc.vector.tensor_tensor(
+                    out=result[:, image, j, cols], in0=acc[image, j][:, cols], in1=pos_b[j][:, cols], op=ADD
                 )
+                nc.sync.dma_start(out=rows[:, j, cols], in_=result[:, image, j, cols])
 
-        b_words = b_rows[:].bitcast(F32)
-        for u in range(2):
-            nc.tensor.transpose(b_turned[:, u, :], b_words[:, u : u + 1].to_broadcast([P, P]), ident[:])
-
-        half = F // 2
-        for h in range(2):
-            cols = slice(h * half, (h + 1) * half)
-            nc.vector.tensor_copy(
-                out=w_grouped[:, cols, :].rearrange("p (c i) t -> p c t i", i=4),
-                in_=w_raw[:, :, cols].rearrange("p t (c i) -> p c t i", i=4),
+        def interleave_w(copy, lo, hi):
+            copy(
+                out=w_grouped[:, lo:hi, :].rearrange("p (c i) t -> p c t i", i=4),
+                in_=w_raw[:, :, lo:hi].rearrange("p t (c i) -> p c t i", i=4),
             )
-        for h in range(2):
-            cols = slice(h * half, (h + 1) * half)
+
+        def quantize_w(h):
+            cols = slice(h * W_HALF, (h + 1) * W_HALF)
             nc.vector.quantize_mx(
                 out=w_codes[:, cols].bitcast(E4M3),
                 scales=w_scales[:, cols],
                 in_=w_grouped[:, cols, :].rearrange("p f t -> p (f t)"),
             )
 
-        for j in range(2):
-            reorder(j)
-            turn(j)
-        for j in range(2):
-            group(j)
-        quantize(0)
-        add_bias(0)
-        nc.scalar.copy(
-            out=b_all[:].bitcast(F32).rearrange("p (n u) -> p n u", u=2),
-            in_=b_turned[:].rearrange("p u n -> p n u"),
-        )
-        reorder(2)
+        reorder(0)
+        turn(0)
+        group(0)
 
-        for j in range(TILES):
-            multiply(j)
-            if j + 2 < TILES:
-                turn(j + 2)
-            if j + 1 < TILES:
-                quantize(j + 1)
-                add_bias(j + 1)
-            if j + 3 < TILES:
-                reorder(j + 3)
-            if j + 2 < TILES:
-                group(j + 2)
-            finish(j)
+        b_words = b_rows[:].bitcast(F32)
+        for u in range(2):
+            nc.tensor.transpose(b_turned[:, u, :], b_words[:, u : u + 1].to_broadcast([P, P]), ident[:])
+
+        interleave_w(nc.vector.tensor_copy, 0, W_HALF)
+        interleave_w(nc.vector.tensor_copy, W_HALF, F)
+        quantize_w(0)
+        quantize(0)
+        quantize_w(1)
+
+        reorder(1)
+        turn(1)
+        add_bias(0)
+
+        for s in range(STEPS):
+            if s + 2 < STEPS:
+                reorder(s + 2)
+                turn(s + 2)
+            multiply(s)
+            if s + 1 < STEPS:
+                group(s + 1)
+                quantize(s + 1)
+            if s == 0:
+                nc.scalar.copy(
+                    out=b_all[:].bitcast(F32).rearrange("p (n u) -> p n u", u=2),
+                    in_=b_turned[:].rearrange("p u n -> p n u"),
+                )
+            if s + 1 < TILES:
+                add_bias(s + 1)
+            for image, j in step_tiles(s):
+                finish(image, j)

from contextlib import ExitStack

import concourse.mybir as mybir
from concourse.masks import make_identity

F32 = mybir.dt.float32
BF16 = mybir.dt.bfloat16
U32 = mybir.dt.uint32
U8 = mybir.dt.uint8
E4M3 = mybir.dt.float8_e4m3fn_x4
E5M2 = mybir.dt.float8_e5m2_x4
ADD = mybir.AluOpType.add

P = 128
IMAGES = 2
TILES = 8
K = 512
F = 512
STEPS = TILES + 1
FLOPS = 2 * IMAGES * TILES * P * K * F

W_HALF = F // 2


def step_tiles(s):
    return [(image, s - image) for image in range(IMAGES) if 0 <= s - image < TILES]


def tile_resampling_kernel(tc, encoded, W, b, pos_emb, out):
    nc = tc.nc
    with ExitStack() as ctx:
        keep = ctx.enter_context(tc.tile_pool(name="keep", bufs=1))
        stage = ctx.enter_context(tc.tile_pool(name="stage", bufs=4))
        pair = ctx.enter_context(tc.tile_pool(name="pair", bufs=3))
        ps_bias = ctx.enter_context(tc.psum_pool(name="ps_bias", bufs=1))
        ps_turn = ctx.enter_context(tc.psum_pool(name="ps_turn", bufs=3))
        ps_acc = ctx.enter_context(tc.psum_pool(name="ps_acc", bufs=4))
        ctx.enter_context(tc.manual_schedule())

        ident = keep.tile([P, P], F32, align_bytes=64)
        b_rows = keep.tile([P, 4], BF16, align_bytes=64)
        b_all = keep.tile([P, F], BF16, align_bytes=64)
        w_raw = keep.tile([P, 4, F], BF16, align_bytes=64)
        w_grouped = keep.tile([P, F, 4], BF16, align_bytes=64)
        w_codes = keep.tile([P, F], U32, align_bytes=64)
        w_scales = keep.tile([P, F], U8, align_bytes=64)
        pos = keep.tile([P, TILES, F], BF16, align_bytes=64)
        result = keep.tile([P, IMAGES, TILES, F], F32, align_bytes=64)
        b_turned = ps_bias.tile([P, 2, P], F32)

        make_identity(nc, ident[:])
        warm = keep.tile([P, 1], F32, align_bytes=64)
        nc.scalar.copy(out=warm[:], in_=ident[:, 0:1])

        w_view = W.rearrange("(p t) f -> p t f", t=4)
        pos_view = pos_emb.rearrange("(p j) f -> p j f", j=TILES)
        x_raw = {}

        def load_x(image, lo, hi):
            raw = keep.tile([P, 2, (hi - lo) * 256], BF16, name="x_raw_%d_%d" % (image, lo), align_bytes=64)
            rows = encoded[image].rearrange("(y a h t) d -> a y h (t d)", y=32, a=2, h=4, t=16)
            for a in range(2):
                nc.sync.dma_start(out=raw[:, a, :], in_=rows[a][:, :, lo * 256 : hi * 256])
            for j in range(lo, hi):
                x_raw[image, j] = raw[:, :, (j - lo) * 256 : (j - lo + 1) * 256]

        def load_pos(lo, hi):
            nc.sync.dma_start(out=pos[:, lo:hi, :], in_=pos_view[:, lo:hi, :])

        load_x(0, 0, 1)
        nc.sync.dma_start(out=w_raw[:], in_=w_view)
        nc.sync.dma_start(out=b_rows[:], in_=b.rearrange("(p c) -> p c", c=4))
        load_x(0, 1, 2)
        load_x(1, 0, 1)
        load_x(0, 2, 3)
        load_x(1, 1, 2)
        load_pos(0, 2)
        load_x(0, 3, 5)
        load_x(1, 2, 4)
        load_pos(2, 4)
        load_x(0, 5, 8)
        load_x(1, 4, 8)
        load_pos(4, 8)

        ordered = {}
        turned = {}
        grouped = {}
        codes = {}
        scales = {}
        acc = {}
        pos_b = {}

        def reorder(s):
            t = stage.tile([P, IMAGES, 2, P], F32, name="ordered", align_bytes=64)
            ordered[s] = t
            for d, key in enumerate(step_tiles(s)):
                words = x_raw[key].bitcast(F32).rearrange("p a (c r q u) -> p u a r c q", c=2, r=8, u=2)
                for u in range(2):
                    nc.scalar.copy(out=t[:, d, u, :].rearrange("p (a r c q) -> p a r c q", a=2, r=8, c=2), in_=words[:, u])

        def turn(s):
            t = ps_turn.tile([P, IMAGES, 2, P], F32, name="turned")
            turned[s] = t
            for d in range(len(step_tiles(s))):
                for u in range(2):
                    nc.tensor.transpose(t[:, d, u, :], ordered[s][:, d, u, :], ident[:])

        def group(s):
            n = len(step_tiles(s))
            t = stage.tile([P, IMAGES * P * 4], BF16, name="grouped", align_bytes=64)
            grouped[s] = t[:, : n * P * 4]
            dst = grouped[s].bitcast(F32).rearrange("p (d m u) -> p d m u", d=n, u=2)
            nc.scalar.copy(out=dst, in_=turned[s][:, :n, :, :].rearrange("p d u m -> p d m u"))

        def quantize(s):
            n = len(step_tiles(s))
            c = stage.tile([P, IMAGES * P], U32, name="x_codes", align_bytes=64)
            e = stage.tile([P, IMAGES * P], U8, name="x_scales", align_bytes=64)
            codes[s] = c
            scales[s] = e
            nc.vector.quantize_mx(out=c[:, : n * P].bitcast(E5M2), scales=e[:, : n * P], in_=grouped[s])

        def multiply(s):
            for d, key in enumerate(step_tiles(s)):
                t = ps_acc.tile([P, F], F32, name="acc")
                acc[key] = t
                cols = slice(d * P, (d + 1) * P)
                nc.tensor.matmul_mx(
                    out=t[:],
                    lhsT=codes[s][:, cols].bitcast(E5M2),
                    lhsT_scale=scales[s][:, cols],
                    rhs=w_codes[:].bitcast(E4M3),
                    rhs_scale=w_scales[:],
                    start=True,
                    stop=True,
                )

        def add_bias(j):
            t = pair.tile([P, F], F32, name="pos_b", align_bytes=64)
            pos_b[j] = t
            if j == 0:
                nc.vector.tensor_tensor(
                    out=t[:].rearrange("p (n u e) -> p n u e", u=2, e=2),
                    in0=pos[:, j, :].rearrange("p (n u e) -> p n u e", u=2, e=2),
                    in1=b_turned[:].bitcast(BF16).rearrange("p u (n e) -> p n u e", e=2),
                    op=ADD,
                )
            else:
                nc.gpsimd.tensor_tensor(out=t[:], in0=pos[:, j, :], in1=b_all[:], op=ADD)

        def finish(image, j):
            rows = out[image].rearrange("(p j) f -> p j f", j=TILES)
            parts = 2 if (image, j) == (IMAGES - 1, TILES - 1) else 1
            for part in range(parts):
                cols = slice(part * F // parts, (part + 1) * F // parts)
                nc.vector.tensor_tensor(
                    out=result[:, image, j, cols], in0=acc[image, j][:, cols], in1=pos_b[j][:, cols], op=ADD
                )
                nc.sync.dma_start(out=rows[:, j, cols], in_=result[:, image, j, cols])

        def interleave_w(copy, lo, hi):
            copy(
                out=w_grouped[:, lo:hi, :].rearrange("p (c i) t -> p c t i", i=4),
                in_=w_raw[:, :, lo:hi].rearrange("p t (c i) -> p c t i", i=4),
            )

        def quantize_w(h):
            cols = slice(h * W_HALF, (h + 1) * W_HALF)
            nc.vector.quantize_mx(
                out=w_codes[:, cols].bitcast(E4M3),
                scales=w_scales[:, cols],
                in_=w_grouped[:, cols, :].rearrange("p f t -> p (f t)"),
            )

        reorder(0)
        turn(0)
        group(0)

        b_words = b_rows[:].bitcast(F32)
        for u in range(2):
            nc.tensor.transpose(b_turned[:, u, :], b_words[:, u : u + 1].to_broadcast([P, P]), ident[:])

        interleave_w(nc.vector.tensor_copy, 0, W_HALF)
        interleave_w(nc.vector.tensor_copy, W_HALF, F)
        quantize_w(0)
        quantize(0)
        quantize_w(1)

        reorder(1)
        turn(1)
        add_bias(0)

        for s in range(STEPS):
            if s + 2 < STEPS:
                reorder(s + 2)
                turn(s + 2)
            multiply(s)
            if s + 1 < STEPS:
                group(s + 1)
                quantize(s + 1)
            if s == 0:
                nc.scalar.copy(
                    out=b_all[:].bitcast(F32).rearrange("p (n u) -> p n u", u=2),
                    in_=b_turned[:].rearrange("p u n -> p n u"),
                )
            if s + 1 < TILES:
                add_bias(s + 1)
            for image, j in step_tiles(s):
                finish(image, j)
